import numpy as np
import ml_dtypes


def mxq(x, axis, fmt="e4m3"):
    dtype, down = {"e4m3": (ml_dtypes.float8_e4m3fn, 7), "e5m2": (ml_dtypes.float8_e5m2, 14)}[fmt]
    v = np.moveaxis(np.asarray(x, np.float32).astype(ml_dtypes.bfloat16).astype(np.float64), axis, -1)
    blocks = v.reshape(v.shape[:-1] + (-1, 32))
    amax = np.abs(blocks).max(-1, keepdims=True)
    byte = np.maximum(np.where(amax > 0, np.frexp(amax)[1] - 1 + 127, 0) - down, 1)
    scale = np.exp2(byte - 127.0)
    codes = (blocks / scale).astype(np.float32).astype(dtype).astype(np.float64)
    return np.moveaxis((codes * scale).reshape(v.shape), -1, axis)


WIDE = False


def mx_kscale(k):
    if not WIDE:
        return np.ones(k)
    levels = np.array([10, -10, 5, -5, 0])
    a = np.random.permutation(np.resize(levels, k // 512 * 4)).reshape(k // 512, 4)
    idx = np.arange(k)
    return np.exp2(a[idx // 512, idx % 128 // 32])


BF16 = ml_dtypes.bfloat16


def bf(x):
    return np.asarray(x, np.float32).astype(BF16)


def f64(x):
    return np.asarray(x).astype(np.float64)


E2M1 = np.array([0.0, 0.5, 1.0, 1.5, 2.0, 3.0, 4.0, 6.0, -0.0, -0.5, -1.0, -1.5, -2.0, -3.0, -4.0, -6.0])


def pack_weight(w, fmt):
    k, n = w.shape
    w = f64(bf(w)).reshape(k // 32, 32, n)
    amax = np.abs(w).max(1)
    if fmt == "e4m3":
        byte = np.frexp(amax)[1] - 1 + 127 - 7
    else:
        mant, ex = np.frexp(amax / 6.0)
        byte = np.where(mant > 0.5, ex, ex - 1) + 127
    byte = np.clip(np.where(amax > 0, byte, 1), 1, 254)
    scaled = (w * np.exp2(127.0 - byte)[:, None, :]).reshape(k, n).astype(np.float32)
    by_word = np.ascontiguousarray(scaled.reshape(k // 512, 128, 4, n).transpose(0, 1, 3, 2))
    if fmt == "e4m3":
        words = by_word.astype(ml_dtypes.float8_e4m3fn).view(np.uint8)
    else:
        c = by_word.astype(ml_dtypes.float4_e2m1fn).view(np.uint8) & 0xF
        words = c[..., 0::2] | (c[..., 1::2] << 4)
    return np.ascontiguousarray(words), np.ascontiguousarray(byte.astype(np.uint8).reshape(k // 512, 16, n))


def unpack_weight(words, scales, fmt):
    g, p, n, _ = words.shape
    if fmt == "e4m3":
        vals = np.ascontiguousarray(words).view(ml_dtypes.float8_e4m3fn).astype(np.float64)
    else:
        nib = np.empty((g, p, n, 4), np.uint8)
        nib[..., 0::2] = words & 0xF
        nib[..., 1::2] = words >> 4
        vals = E2M1[nib]
    vals = vals * np.repeat(np.exp2(scales.astype(np.float64) - 127.0), 8, axis=1)[..., None]
    return vals.transpose(0, 1, 3, 2).reshape(g * 512, n)

def pack4(w):
    words, scales = pack_weight(w, "e2m1")
    return words.reshape(words.shape[0], 128, -1), scales


def unpack4(words, scales):
    return unpack_weight(words.reshape(words.shape[0], 128, -1, 2), scales, "e2m1")


B, T, D, H = 4, 1024, 1024, 8
HD = D // H
SCALE = HD ** (-0.5)


def rotate_half(u):
    u1, u2 = np.split(u, 2, axis=-1)
    return np.concatenate([-u2, u1], axis=-1)


def apply_rope(u, sin, cos):
    return u * cos[None, :, None, :] + rotate_half(u) * sin[None, :, None, :]


def setup_inputs():
    s = mx_kscale(D)
    x = bf(np.random.standard_normal((B, T, D)) * s)
    sin = bf(np.random.standard_normal((T, HD)))
    cos = bf(np.random.standard_normal((T, HD)))
    words, scales = pack4(np.random.standard_normal((D, D + 2 * HD)) * 2.0 / np.sqrt(D) / s[:, None])
    return {"x": x,
            "sin": sin,
            "cos": cos,
            "W_qkv_words": words,
            "W_qkv_scales": scales}


def reference(x, sin, cos, W_qkv_words, W_qkv_scales):
    sin, cos = f64(sin), f64(cos)
    qkv = mxq(f64(x), 2, "e4m3") @ unpack4(W_qkv_words, W_qkv_scales)
    q, k, v = np.split(qkv, [D, D + HD], axis=-1)
    q = q.reshape(B, T, H, HD) * SCALE
    q_rot = np.ascontiguousarray(apply_rope(q, sin, cos).transpose(0, 2, 1, 3))
    k_rot = apply_rope(k[:, :, None, :], sin, cos)[:, :, 0, :]
    return q_rot, k_rot, v

@@ -1,0 +1,241 @@
+from contextlib import ExitStack
+
+import concourse.mybir as mybir
+from concourse.masks import make_identity
+
+F32 = mybir.dt.float32
+BF16 = mybir.dt.bfloat16
+U8 = mybir.dt.uint8
+U32 = mybir.dt.uint32
+I32 = mybir.dt.int32
+FP8X4 = mybir.dt.float8_e4m3fn_x4
+FP4X4 = mybir.dt.float4_e2m1fn_x4
+MULT = mybir.AluOpType.mult
+ADD = mybir.AluOpType.add
+COPY = mybir.ActivationFunctionType.Copy
+
+P = 128
+B, T, D, H = 4, 1024, 1024, 8
+HD = D // H
+HALF = HD // 2
+N_QKV = D + 2 * HD
+Q_SCALE = HD ** (-0.5)
+K_PASS = 4 * P
+PASSES = D // K_PASS
+ROWS = T // P
+TILES = B * ROWS
+PAIR = 2
+ROPE_HEADS = H + 1
+V_SLOT = ROPE_HEADS
+
+FLOPS = 2 * B * T * D * N_QKV
+
+BANK_A = (0, 4)
+BANK_B = (4, 2)
+BANK_C = (6, 4)
+
+
+def tile_multiqueryattention_pa_t_kernel(
+    tc, x, sin, cos, W_qkv_words, W_qkv_scales, out_0, out_1, out_2
+):
+    nc = tc.nc
+    with ExitStack() as ctx:
+        keep = ctx.enter_context(tc.tile_pool(name="keep", bufs=1))
+        quant = ctx.enter_context(tc.tile_pool(name="quant", bufs=4))
+        work = ctx.enter_context(tc.tile_pool(name="work", bufs=3))
+        psum = ctx.enter_context(tc.psum_pool(name="psum", bufs=2))
+        ctx.enter_context(tc.manual_schedule())
+
+        w_scales = keep.tile([P, PASSES, N_QKV], U8, align_bytes=64)
+        nc.vector.memset(w_scales[:].bitcast(I32), 0)
+
+        sin_bf = keep.tile([P, ROWS, HD], BF16)
+        cos_bf = keep.tile([P, ROWS, HD], BF16)
+        nc.sync.dma_start(out=sin_bf[:], in_=sin.rearrange("(p j) d -> p j d", j=ROWS))
+        nc.sync.dma_start(out=cos_bf[:], in_=cos.rearrange("(p j) d -> p j d", j=ROWS))
+
+        x_pairs = []
+
+        def load_x_pair(s):
+            b, j = divmod(PAIR * s, ROWS)
+            x_sb = keep.tile([P, PAIR, D], BF16, name="x_sb%d" % s)
+            nc.sync.dma_start(
+                out=x_sb[:], in_=x[b].rearrange("(p j) k -> p j k", j=ROWS)[:, j : j + PAIR, :]
+            )
+            x_pairs.append(x_sb)
+
+        load_x_pair(0)
+
+        scale_rows = W_qkv_scales.bitcast(I32).rearrange("g q n -> q g n")
+        for quadrant in range(4):
+            nc.sync.dma_start(
+                out=w_scales[32 * quadrant : 32 * quadrant + 4].bitcast(I32),
+                in_=scale_rows[4 * quadrant : 4 * quadrant + 4],
+            )
+        w_words = keep.tile([P, PASSES, 2 * N_QKV], U8, align_bytes=64)
+        nc.sync.dma_start(
+            out=w_words[:].bitcast(I32), in_=W_qkv_words.bitcast(I32).rearrange("g p n -> p g n")
+        )
+        for s in range(1, TILES // PAIR):
+            load_x_pair(s)
+
+        ident = keep.tile([P, P], F32)
+        make_identity(nc, ident[:])
+
+        cos_tab = keep.tile([P, ROWS, 3, HD], F32)
+        sin_tab = keep.tile([P, ROWS, 3, HD], F32)
+
+        def build_tables(j0, j1):
+            n = j1 - j0
+            nc.scalar.activation(
+                out=cos_tab[:, j0:j1, 0:2, :],
+                in_=cos_bf[:, j0:j1, :].unsqueeze(2).to_broadcast([P, n, 2, HD]),
+                func=COPY,
+                scale=Q_SCALE,
+            )
+            nc.scalar.copy(out=cos_tab[:, j0:j1, 2, :], in_=cos_bf[:, j0:j1, :])
+            for lo, other, sign in ((0, HALF, 1.0), (HALF, 0, -1.0)):
+                nc.gpsimd.tensor_scalar(
+                    out=sin_tab[:, j0:j1, 0:2, lo : lo + HALF],
+                    in0=sin_bf[:, j0:j1, other : other + HALF].unsqueeze(2).to_broadcast([P, n, 2, HALF]),
+                    scalar1=sign * Q_SCALE,
+                    scalar2=0.0,
+                    op0=MULT,
+                    op1=ADD,
+                )
+                nc.gpsimd.tensor_scalar(
+                    out=sin_tab[:, j0:j1, 2, lo : lo + HALF],
+                    in0=sin_bf[:, j0:j1, other : other + HALF],
+                    scalar1=sign,
+                    scalar2=0.0,
+                    op0=MULT,
+                    op1=ADD,
+                )
+
+        grouped_of = {}
+        codes_of = {}
+        banks_of = {}
+        out_of = {}
+
+        def transpose_tile(i):
+            x_words = x_pairs[i // PAIR][:, i % PAIR, :].bitcast(F32)
+            xt = psum.tile([P, 2 * PASSES, P], F32)
+            for g in range(PASSES):
+                for u in range(2):
+                    nc.tensor.transpose(
+                        xt[:, 2 * g + u, :], x_words[:, 256 * g + u : 256 * (g + 1) : 2], ident[:]
+                    )
+            grouped = quant.tile([P, PASSES, P, 4], BF16, align_bytes=64)
+            nc.scalar.copy(
+                out=grouped[:]
+                .rearrange("p g r t -> p (g r t)")
+                .bitcast(F32)
+                .rearrange("p (g r u) -> p g r u", g=PASSES, u=2),
+                in_=xt[:].rearrange("p (g u) r -> p g r u", u=2),
+            )
+            grouped_of[i] = grouped
+
+        def quantise_tile(i):
+            codes = quant.tile([P, PASSES, P], U32, align_bytes=64)
+            scales = quant.tile([P, PASSES, P], U8, align_bytes=64)
+            nc.vector.quantize_mx(
+                out=codes[:].rearrange("p g r -> p (g r)").bitcast(FP8X4),
+                scales=scales[:].rearrange("p g r -> p (g r)"),
+                in_=grouped_of[i][:].rearrange("p g r t -> p (g r t)"),
+            )
+            codes_of[i] = (codes, scales)
+
+        def project(codes, scales, acc, col0, width):
+            for g in range(PASSES):
+                nc.tensor.matmul_mx(
+                    out=acc,
+                    lhsT=codes[:, g, :].bitcast(FP8X4),
+                    lhsT_scale=scales[:, g, :],
+                    rhs=w_words[:, g, 2 * col0 : 2 * (col0 + width)].bitcast(FP4X4),
+                    rhs_scale=w_scales[:, g, col0 : col0 + width],
+                    start=(g == 0),
+                    stop=(g == PASSES - 1),
+                )
+
+        def project_tile(i):
+            codes, scales = codes_of[i]
+            bank_a = psum.tile([P, BANK_A[1], HD], F32)
+            bank_b = psum.tile([P, BANK_B[1], HD], F32)
+            bank_c = psum.tile([P, BANK_C[1], HD], F32)
+            project(codes, scales, bank_a[:].rearrange("p h d -> p (h d)"), BANK_A[0] * HD, BANK_A[1] * HD)
+            for h in range(BANK_B[1]):
+                project(codes, scales, bank_b[:, h, :], (BANK_B[0] + h) * HD, HD)
+            project(codes, scales, bank_c[:].rearrange("p h d -> p (h d)"), BANK_C[0] * HD, BANK_C[1] * HD)
+            banks_of[i] = (bank_a, bank_b, bank_c)
+
+        def open_pair(s):
+            first = work.tile([P, ROPE_HEADS + 1, PAIR, HD], F32)
+            second = work.tile([P, ROPE_HEADS, PAIR, HD], F32)
+            out_of[s] = (first, second)
+
+        def copy_value_head(i):
+            first = out_of[i // PAIR][0]
+            bank_c = banks_of[i][2]
+            nc.scalar.copy(out=first[:, V_SLOT, i % PAIR, :], in_=bank_c[:, V_SLOT - BANK_C[0], :])
+
+        def rope_tile(i):
+            j = i % ROWS
+            jj = i % PAIR
+            first, second = out_of[i // PAIR]
+            bank_a, bank_b, bank_c = banks_of[i]
+            for table, dest in ((cos_tab, first), (sin_tab, second)):
+                for bank, (h0, n) in ((bank_a, BANK_A), (bank_b, BANK_B)):
+                    nc.vector.tensor_tensor(
+                        out=dest[:, h0 : h0 + n, jj, :],
+                        in0=bank[:],
+                        in1=table[:, j, 0, :].unsqueeze(1).to_broadcast([P, n, HD]),
+                        op=MULT,
+                    )
+                nc.vector.tensor_tensor(
+                    out=dest[:, BANK_C[0] : ROPE_HEADS, jj, :],
+                    in0=bank_c[:, 0:3, :],
+                    in1=table[:, j, :, :],
+                    op=MULT,
+                )
+
+        def finish_pair(s):
+            b, j = divmod(PAIR * s, ROWS)
+            first, second = out_of[s]
+            for lo, other in ((0, HALF), (HALF, 0)):
+                nc.gpsimd.tensor_tensor(
+                    out=first[:, 0:ROPE_HEADS, :, lo : lo + HALF],
+                    in0=first[:, 0:ROPE_HEADS, :, lo : lo + HALF],
+                    in1=second[:, :, :, other : other + HALF],
+                    op=ADD,
+                )
+            nc.sync.dma_start(
+                out=out_0[b].rearrange("h (p j) d -> p h j d", j=ROWS)[:, :, j : j + PAIR, :],
+                in_=first[:, 0:H, :, :],
+            )
+            nc.sync.dma_start(
+                out=out_1[b].rearrange("(p j) d -> p j d", j=ROWS)[:, j : j + PAIR, :],
+                in_=first[:, H, :, :],
+            )
+            nc.sync.dma_start(
+                out=out_2[b].rearrange("(p j) d -> p j d", j=ROWS)[:, j : j + PAIR, :],
+                in_=first[:, V_SLOT, :, :],
+            )
+
+        build_tables(0, ROWS // 2)
+        for i in range(3):
+            transpose_tile(i)
+        build_tables(ROWS // 2, ROWS)
+        for i in range(2):
+            quantise_tile(i)
+        for i in range(TILES):
+            if i + 2 < TILES:
+                quantise_tile(i + 2)
+            if i % PAIR == 0:
+                open_pair(i // PAIR)
+            project_tile(i)
+            copy_value_head(i)
+            if i + 3 < TILES:
+                transpose_tile(i + 3)
+            rope_tile(i)
+            if i % PAIR == PAIR - 1:
+                finish_pair(i // PAIR)

@@ -82,21 +82,20 @@ def tile_multiqueryattention_pa_t_kernel(
         ident = keep.tile([P, P], F32)
         make_identity(nc, ident[:])
 
-        cos_tab = keep.tile([P, ROWS, 3, HD], F32)
-        sin_tab = keep.tile([P, ROWS, 3, HD], F32)
+        tables = keep.tile([P, ROWS, 2, 3, HD], F32)
 
         def build_tables(j0, j1):
             n = j1 - j0
             nc.scalar.activation(
-                out=cos_tab[:, j0:j1, 0:2, :],
+                out=tables[:, j0:j1, 0, 0:2, :],
                 in_=cos_bf[:, j0:j1, :].unsqueeze(2).to_broadcast([P, n, 2, HD]),
                 func=COPY,
                 scale=Q_SCALE,
             )
-            nc.scalar.copy(out=cos_tab[:, j0:j1, 2, :], in_=cos_bf[:, j0:j1, :])
+            nc.scalar.copy(out=tables[:, j0:j1, 0, 2, :], in_=cos_bf[:, j0:j1, :])
             for lo, other, sign in ((0, HALF, 1.0), (HALF, 0, -1.0)):
                 nc.gpsimd.tensor_scalar(
-                    out=sin_tab[:, j0:j1, 0:2, lo : lo + HALF],
+                    out=tables[:, j0:j1, 1, 0:2, lo : lo + HALF],
                     in0=sin_bf[:, j0:j1, other : other + HALF].unsqueeze(2).to_broadcast([P, n, 2, HALF]),
                     scalar1=sign * Q_SCALE,
                     scalar2=0.0,
@@ -104,7 +103,7 @@ def tile_multiqueryattention_pa_t_kernel(
                     op1=ADD,
                 )
                 nc.gpsimd.tensor_scalar(
-                    out=sin_tab[:, j0:j1, 2, lo : lo + HALF],
+                    out=tables[:, j0:j1, 1, 2, lo : lo + HALF],
                     in0=sin_bf[:, j0:j1, other : other + HALF],
                     scalar1=sign,
                     scalar2=0.0,
@@ -169,56 +168,54 @@ def tile_multiqueryattention_pa_t_kernel(
             banks_of[i] = (bank_a, bank_b, bank_c)
 
         def open_pair(s):
-            first = work.tile([P, ROPE_HEADS + 1, PAIR, HD], F32)
-            second = work.tile([P, ROPE_HEADS, PAIR, HD], F32)
-            out_of[s] = (first, second)
+            products = work.tile([P, 2, ROPE_HEADS + 1, PAIR, HD], F32)
+            out_of[s] = products
 
         def copy_value_head(i):
-            first = out_of[i // PAIR][0]
             bank_c = banks_of[i][2]
-            nc.scalar.copy(out=first[:, V_SLOT, i % PAIR, :], in_=bank_c[:, V_SLOT - BANK_C[0], :])
+            nc.scalar.copy(
+                out=out_of[i // PAIR][:, 0, V_SLOT, i % PAIR, :], in_=bank_c[:, V_SLOT - BANK_C[0], :]
+            )
 
         def rope_tile(i):
             j = i % ROWS
-            jj = i % PAIR
-            first, second = out_of[i // PAIR]
+            products = out_of[i // PAIR]
             bank_a, bank_b, bank_c = banks_of[i]
-            for table, dest in ((cos_tab, first), (sin_tab, second)):
-                for bank, (h0, n) in ((bank_a, BANK_A), (bank_b, BANK_B)):
-                    nc.vector.tensor_tensor(
-                        out=dest[:, h0 : h0 + n, jj, :],
-                        in0=bank[:],
-                        in1=table[:, j, 0, :].unsqueeze(1).to_broadcast([P, n, HD]),
-                        op=MULT,
-                    )
+            for bank, (h0, n) in ((bank_a, BANK_A), (bank_b, BANK_B)):
                 nc.vector.tensor_tensor(
-                    out=dest[:, BANK_C[0] : ROPE_HEADS, jj, :],
-                    in0=bank_c[:, 0:3, :],
-                    in1=table[:, j, :, :],
+                    out=products[:, :, h0 : h0 + n, i % PAIR, :],
+                    in0=bank[:].unsqueeze(1).to_broadcast([P, 2, n, HD]),
+                    in1=tables[:, j, :, 0, :].unsqueeze(2).to_broadcast([P, 2, n, HD]),
                     op=MULT,
                 )
+            nc.vector.tensor_tensor(
+                out=products[:, :, BANK_C[0] : ROPE_HEADS, i % PAIR, :],
+                in0=bank_c[:, 0:3, :].unsqueeze(1).to_broadcast([P, 2, 3, HD]),
+                in1=tables[:, j, :, :, :],
+                op=MULT,
+            )
 
-        def finish_pair(s):
+        def finish_pair(s, adder):
             b, j = divmod(PAIR * s, ROWS)
-            first, second = out_of[s]
+            products = out_of[s]
             for lo, other in ((0, HALF), (HALF, 0)):
-                nc.gpsimd.tensor_tensor(
-                    out=first[:, 0:ROPE_HEADS, :, lo : lo + HALF],
-                    in0=first[:, 0:ROPE_HEADS, :, lo : lo + HALF],
-                    in1=second[:, :, :, other : other + HALF],
+                adder.tensor_tensor(
+                    out=products[:, 0, 0:ROPE_HEADS, :, lo : lo + HALF],
+                    in0=products[:, 0, 0:ROPE_HEADS, :, lo : lo + HALF],
+                    in1=products[:, 1, 0:ROPE_HEADS, :, other : other + HALF],
                     op=ADD,
                 )
             nc.sync.dma_start(
                 out=out_0[b].rearrange("h (p j) d -> p h j d", j=ROWS)[:, :, j : j + PAIR, :],
-                in_=first[:, 0:H, :, :],
+                in_=products[:, 0, 0:H, :, :],
             )
             nc.sync.dma_start(
                 out=out_1[b].rearrange("(p j) d -> p j d", j=ROWS)[:, j : j + PAIR, :],
-                in_=first[:, H, :, :],
+                in_=products[:, 0, H, :, :],
             )
             nc.sync.dma_start(
                 out=out_2[b].rearrange("(p j) d -> p j d", j=ROWS)[:, j : j + PAIR, :],
-                in_=first[:, V_SLOT, :, :],
+                in_=products[:, 0, V_SLOT, :, :],
             )
 
         build_tables(0, ROWS // 2)
@@ -238,4 +235,4 @@ def tile_multiqueryattention_pa_t_kernel(
                 transpose_tile(i + 3)
             rope_tile(i)
             if i % PAIR == PAIR - 1:
-                finish_pair(i // PAIR)
+                finish_pair(i // PAIR, nc.vector if i == TILES - 1 else nc.gpsimd)

@@ -25,6 +25,7 @@ PASSES = D // K_PASS
 ROWS = T // P
 TILES = B * ROWS
 PAIR = 2
+VECTOR_ADD_TILES = 3
 ROPE_HEADS = H + 1
 V_SLOT = ROPE_HEADS
 
@@ -42,7 +43,7 @@ def tile_multiqueryattention_pa_t_kernel(
     with ExitStack() as ctx:
         keep = ctx.enter_context(tc.tile_pool(name="keep", bufs=1))
         quant = ctx.enter_context(tc.tile_pool(name="quant", bufs=4))
-        work = ctx.enter_context(tc.tile_pool(name="work", bufs=3))
+        work = ctx.enter_context(tc.tile_pool(name="work", bufs=4))
         psum = ctx.enter_context(tc.psum_pool(name="psum", bufs=2))
         ctx.enter_context(tc.manual_schedule())
 
@@ -195,27 +196,26 @@ def tile_multiqueryattention_pa_t_kernel(
                 op=MULT,
             )
 
-        def finish_pair(s, adder):
-            b, j = divmod(PAIR * s, ROWS)
-            products = out_of[s]
-            for lo, other in ((0, HALF), (HALF, 0)):
-                adder.tensor_tensor(
-                    out=products[:, 0, 0:ROPE_HEADS, :, lo : lo + HALF],
-                    in0=products[:, 0, 0:ROPE_HEADS, :, lo : lo + HALF],
-                    in1=products[:, 1, 0:ROPE_HEADS, :, other : other + HALF],
-                    op=ADD,
-                )
+        def add_tile(i, adder):
+            products = out_of[i // PAIR]
+            first = products[:, 0, 0:ROPE_HEADS, i % PAIR, :].rearrange("p h (e c) -> p h e c", e=2)
+            second = products[:, 1, 0:ROPE_HEADS, i % PAIR, :].rearrange("p h (e c) -> p h e c", e=2)
+            adder.tensor_tensor(out=first, in0=first, in1=second[:, :, ::-1, :], op=ADD)
+
+        def store_tiles(i0, n):
+            b, j = divmod(i0, ROWS)
+            jj = i0 % PAIR
+            outputs = out_of[i0 // PAIR][:, 0, :, jj : jj + n, :]
             nc.sync.dma_start(
-                out=out_0[b].rearrange("h (p j) d -> p h j d", j=ROWS)[:, :, j : j + PAIR, :],
-                in_=products[:, 0, 0:H, :, :],
+                out=out_0[b].rearrange("h (p j) d -> p h j d", j=ROWS)[:, :, j : j + n, :],
+                in_=outputs[:, 0:H, :, :],
             )
             nc.sync.dma_start(
-                out=out_1[b].rearrange("(p j) d -> p j d", j=ROWS)[:, j : j + PAIR, :],
-                in_=products[:, 0, H, :, :],
+                out=out_1[b].rearrange("(p j) d -> p j d", j=ROWS)[:, j : j + n, :], in_=outputs[:, H, :, :]
             )
             nc.sync.dma_start(
-                out=out_2[b].rearrange("(p j) d -> p j d", j=ROWS)[:, j : j + PAIR, :],
-                in_=products[:, 0, V_SLOT, :, :],
+                out=out_2[b].rearrange("(p j) d -> p j d", j=ROWS)[:, j : j + n, :],
+                in_=outputs[:, V_SLOT, :, :],
             )
 
         build_tables(0, ROWS // 2)
@@ -234,5 +234,8 @@ def tile_multiqueryattention_pa_t_kernel(
             if i + 3 < TILES:
                 transpose_tile(i + 3)
             rope_tile(i)
-            if i % PAIR == PAIR - 1:
-                finish_pair(i // PAIR, nc.vector if i == TILES - 1 else nc.gpsimd)
+            add_tile(i, nc.vector if i >= TILES - VECTOR_ADD_TILES else nc.gpsimd)
+            if i >= TILES - PAIR:
+                store_tiles(i, 1)
+            elif i % PAIR == PAIR - 1:
+                store_tiles(i - PAIR + 1, PAIR)

@@ -25,7 +25,7 @@ PASSES = D // K_PASS
 ROWS = T // P
 TILES = B * ROWS
 PAIR = 2
-VECTOR_ADD_TILES = 3
+VECTOR_ADD_TILES = 1
 ROPE_HEADS = H + 1
 V_SLOT = ROPE_HEADS
 

@@ -25,6 +25,7 @@ PASSES = D // K_PASS
 ROWS = T // P
 TILES = B * ROWS
 PAIR = 2
+FIRST_ROWS = 2
 VECTOR_ADD_TILES = 1
 ROPE_HEADS = H + 1
 V_SLOT = ROPE_HEADS
@@ -52,20 +53,28 @@ def tile_multiqueryattention_pa_t_kernel(
 
         sin_bf = keep.tile([P, ROWS, HD], BF16)
         cos_bf = keep.tile([P, ROWS, HD], BF16)
-        nc.sync.dma_start(out=sin_bf[:], in_=sin.rearrange("(p j) d -> p j d", j=ROWS))
-        nc.sync.dma_start(out=cos_bf[:], in_=cos.rearrange("(p j) d -> p j d", j=ROWS))
+
+        def load_table_rows(j0, j1):
+            for table_bf, table in ((cos_bf, cos), (sin_bf, sin)):
+                nc.sync.dma_start(
+                    out=table_bf[:, j0:j1, :], in_=table.rearrange("(p j) d -> p j d", j=ROWS)[:, j0:j1, :]
+                )
 
         x_pairs = []
 
-        def load_x_pair(s):
+        def load_x_pair(s, pieces):
             b, j = divmod(PAIR * s, ROWS)
             x_sb = keep.tile([P, PAIR, D], BF16, name="x_sb%d" % s)
-            nc.sync.dma_start(
-                out=x_sb[:], in_=x[b].rearrange("(p j) k -> p j k", j=ROWS)[:, j : j + PAIR, :]
-            )
             x_pairs.append(x_sb)
+            n = PAIR // pieces
+            return [
+                (x_sb[:, a : a + n, :], x[b].rearrange("(p j) k -> p j k", j=ROWS)[:, j + a : j + a + n, :])
+                for a in range(0, PAIR, n)
+            ]
 
-        load_x_pair(0)
+        load_table_rows(0, FIRST_ROWS)
+        first_x = load_x_pair(0, PAIR)
+        nc.sync.dma_start(out=first_x[0][0], in_=first_x[0][1])
 
         scale_rows = W_qkv_scales.bitcast(I32).rearrange("g q n -> q g n")
         for quadrant in range(4):
@@ -77,24 +86,29 @@ def tile_multiqueryattention_pa_t_kernel(
         nc.sync.dma_start(
             out=w_words[:].bitcast(I32), in_=W_qkv_words.bitcast(I32).rearrange("g p n -> p g n")
         )
+        nc.sync.dma_start(out=first_x[1][0], in_=first_x[1][1])
+        load_table_rows(FIRST_ROWS, ROWS)
         for s in range(1, TILES // PAIR):
-            load_x_pair(s)
+            for sb_side, hbm_side in load_x_pair(s, 1):
+                nc.sync.dma_start(out=sb_side, in_=hbm_side)
 
         ident = keep.tile([P, P], F32)
         make_identity(nc, ident[:])
 
         tables = keep.tile([P, ROWS, 2, 3, HD], F32)
 
-        def build_tables(j0, j1):
+        def sin_halves():
+            return ((0, HALF, 1.0), (HALF, 0, -1.0))
+
+        def build_first_tables(j0, j1):
             n = j1 - j0
-            nc.scalar.activation(
+            nc.vector.tensor_scalar_mul(
                 out=tables[:, j0:j1, 0, 0:2, :],
-                in_=cos_bf[:, j0:j1, :].unsqueeze(2).to_broadcast([P, n, 2, HD]),
-                func=COPY,
-                scale=Q_SCALE,
+                in0=cos_bf[:, j0:j1, :].unsqueeze(2).to_broadcast([P, n, 2, HD]),
+                scalar1=Q_SCALE,
             )
-            nc.scalar.copy(out=tables[:, j0:j1, 0, 2, :], in_=cos_bf[:, j0:j1, :])
-            for lo, other, sign in ((0, HALF, 1.0), (HALF, 0, -1.0)):
+            nc.vector.tensor_copy(out=tables[:, j0:j1, 0, 2, :], in_=cos_bf[:, j0:j1, :])
+            for lo, other, sign in sin_halves():
                 nc.gpsimd.tensor_scalar(
                     out=tables[:, j0:j1, 1, 0:2, lo : lo + HALF],
                     in0=sin_bf[:, j0:j1, other : other + HALF].unsqueeze(2).to_broadcast([P, n, 2, HALF]),
@@ -110,6 +124,29 @@ def tile_multiqueryattention_pa_t_kernel(
                     scalar2=0.0,
                     op0=MULT,
                     op1=ADD,
+                )
+
+        def build_tables(j0, j1):
+            n = j1 - j0
+            nc.scalar.activation(
+                out=tables[:, j0:j1, 0, 0:2, :],
+                in_=cos_bf[:, j0:j1, :].unsqueeze(2).to_broadcast([P, n, 2, HD]),
+                func=COPY,
+                scale=Q_SCALE,
+            )
+            nc.scalar.copy(out=tables[:, j0:j1, 0, 2, :], in_=cos_bf[:, j0:j1, :])
+            for lo, other, sign in sin_halves():
+                nc.scalar.activation(
+                    out=tables[:, j0:j1, 1, 0:2, lo : lo + HALF],
+                    in_=sin_bf[:, j0:j1, other : other + HALF].unsqueeze(2).to_broadcast([P, n, 2, HALF]),
+                    func=COPY,
+                    scale=sign * Q_SCALE,
+                )
+                nc.scalar.activation(
+                    out=tables[:, j0:j1, 1, 2, lo : lo + HALF],
+                    in_=sin_bf[:, j0:j1, other : other + HALF],
+                    func=COPY,
+                    scale=sign,
                 )
 
         grouped_of = {}
@@ -178,7 +215,7 @@ def tile_multiqueryattention_pa_t_kernel(
                 out=out_of[i // PAIR][:, 0, V_SLOT, i % PAIR, :], in_=bank_c[:, V_SLOT - BANK_C[0], :]
             )
 
-        def rope_tile(i):
+        def rope_banks_ab(i):
             j = i % ROWS
             products = out_of[i // PAIR]
             bank_a, bank_b, bank_c = banks_of[i]
@@ -189,6 +226,11 @@ def tile_multiqueryattention_pa_t_kernel(
                     in1=tables[:, j, :, 0, :].unsqueeze(2).to_broadcast([P, 2, n, HD]),
                     op=MULT,
                 )
+
+        def rope_bank_c(i):
+            j = i % ROWS
+            products = out_of[i // PAIR]
+            bank_c = banks_of[i][2]
             nc.vector.tensor_tensor(
                 out=products[:, :, BANK_C[0] : ROPE_HEADS, i % PAIR, :],
                 in0=bank_c[:, 0:3, :].unsqueeze(1).to_broadcast([P, 2, 3, HD]),
@@ -218,22 +260,33 @@ def tile_multiqueryattention_pa_t_kernel(
                 in_=outputs[:, V_SLOT, :, :],
             )
 
-        build_tables(0, ROWS // 2)
-        for i in range(3):
-            transpose_tile(i)
-        build_tables(ROWS // 2, ROWS)
-        for i in range(2):
-            quantise_tile(i)
+        build_first_tables(0, FIRST_ROWS)
+        transpose_tile(0)
+        quantise_tile(0)
+        transposed = 1
+        quantised = 1
+        table_rows = FIRST_ROWS
         for i in range(TILES):
-            if i + 2 < TILES:
-                quantise_tile(i + 2)
+            ready = transposed
+            if i > 0:
+                for t in range(quantised, min(i + 3, ready, quantised + 2, TILES)):
+                    quantise_tile(t)
+                    quantised = t + 1
             if i % PAIR == 0:
                 open_pair(i // PAIR)
             project_tile(i)
             copy_value_head(i)
-            if i + 3 < TILES:
-                transpose_tile(i + 3)
-            rope_tile(i)
+            for t in range(transposed, min(i + 4, transposed + 2, TILES)):
+                transpose_tile(t)
+                transposed = t + 1
+            if table_rows < ROWS:
+                build_tables(table_rows, table_rows + FIRST_ROWS)
+                table_rows += FIRST_ROWS
+            rope_banks_ab(i)
+            if i == 0:
+                quantise_tile(1)
+                quantised = 2
+            rope_bank_c(i)
             add_tile(i, nc.vector if i >= TILES - VECTOR_ADD_TILES else nc.gpsimd)
             if i >= TILES - PAIR:
                 store_tiles(i, 1)

@@ -238,27 +238,32 @@ def tile_multiqueryattention_pa_t_kernel(
                 op=MULT,
             )
 
-        def add_tile(i, adder):
+        def add_heads(i, adder, h0, h1):
             products = out_of[i // PAIR]
-            first = products[:, 0, 0:ROPE_HEADS, i % PAIR, :].rearrange("p h (e c) -> p h e c", e=2)
-            second = products[:, 1, 0:ROPE_HEADS, i % PAIR, :].rearrange("p h (e c) -> p h e c", e=2)
+            first = products[:, 0, h0:h1, i % PAIR, :].rearrange("p h (e c) -> p h e c", e=2)
+            second = products[:, 1, h0:h1, i % PAIR, :].rearrange("p h (e c) -> p h e c", e=2)
             adder.tensor_tensor(out=first, in0=first, in1=second[:, :, ::-1, :], op=ADD)
 
-        def store_tiles(i0, n):
+        def store_queries(i0, n, h0, h1):
             b, j = divmod(i0, ROWS)
             jj = i0 % PAIR
-            outputs = out_of[i0 // PAIR][:, 0, :, jj : jj + n, :]
             nc.sync.dma_start(
-                out=out_0[b].rearrange("h (p j) d -> p h j d", j=ROWS)[:, :, j : j + n, :],
-                in_=outputs[:, 0:H, :, :],
+                out=out_0[b].rearrange("h (p j) d -> p h j d", j=ROWS)[:, h0:h1, j : j + n, :],
+                in_=out_of[i0 // PAIR][:, 0, h0:h1, jj : jj + n, :],
             )
+
+        def store_single_head(i0, n, slot, out_hbm):
+            b, j = divmod(i0, ROWS)
+            jj = i0 % PAIR
             nc.sync.dma_start(
-                out=out_1[b].rearrange("(p j) d -> p j d", j=ROWS)[:, j : j + n, :], in_=outputs[:, H, :, :]
+                out=out_hbm[b].rearrange("(p j) d -> p j d", j=ROWS)[:, j : j + n, :],
+                in_=out_of[i0 // PAIR][:, 0, slot, jj : jj + n, :],
             )
-            nc.sync.dma_start(
-                out=out_2[b].rearrange("(p j) d -> p j d", j=ROWS)[:, j : j + n, :],
-                in_=outputs[:, V_SLOT, :, :],
-            )
+
+        def store_tiles(i0, n):
+            store_queries(i0, n, 0, H)
+            store_single_head(i0, n, H, out_1)
+            store_single_head(i0, n, V_SLOT, out_2)
 
         build_first_tables(0, FIRST_ROWS)
         transpose_tile(0)
@@ -287,8 +292,16 @@ def tile_multiqueryattention_pa_t_kernel(
                 quantise_tile(1)
                 quantised = 2
             rope_bank_c(i)
-            add_tile(i, nc.vector if i >= TILES - VECTOR_ADD_TILES else nc.gpsimd)
-            if i >= TILES - PAIR:
-                store_tiles(i, 1)
-            elif i % PAIR == PAIR - 1:
-                store_tiles(i - PAIR + 1, PAIR)
+            if i < TILES - VECTOR_ADD_TILES:
+                add_heads(i, nc.gpsimd, 0, ROPE_HEADS)
+                if i >= TILES - PAIR:
+                    store_tiles(i, 1)
+                elif i % PAIR == PAIR - 1:
+                    store_tiles(i - PAIR + 1, PAIR)
+            else:
+                store_single_head(i, 1, V_SLOT, out_2)
+                add_heads(i, nc.vector, 0, BANK_C[0])
+                store_queries(i, 1, 0, BANK_C[0])
+                add_heads(i, nc.vector, BANK_C[0], ROPE_HEADS)
+                store_queries(i, 1, BANK_C[0], H)
+                store_single_head(i, 1, H, out_1)

from contextlib import ExitStack

import concourse.mybir as mybir
from concourse.masks import make_identity

F32 = mybir.dt.float32
BF16 = mybir.dt.bfloat16
U8 = mybir.dt.uint8
U32 = mybir.dt.uint32
I32 = mybir.dt.int32
FP8X4 = mybir.dt.float8_e4m3fn_x4
FP4X4 = mybir.dt.float4_e2m1fn_x4
MULT = mybir.AluOpType.mult
ADD = mybir.AluOpType.add
COPY = mybir.ActivationFunctionType.Copy

P = 128
B, T, D, H = 4, 1024, 1024, 8
HD = D // H
HALF = HD // 2
N_QKV = D + 2 * HD
Q_SCALE = HD ** (-0.5)
K_PASS = 4 * P
PASSES = D // K_PASS
ROWS = T // P
TILES = B * ROWS
PAIR = 2
FIRST_ROWS = 2
VECTOR_ADD_TILES = 1
ROPE_HEADS = H + 1
V_SLOT = ROPE_HEADS

FLOPS = 2 * B * T * D * N_QKV

BANK_A = (0, 4)
BANK_B = (4, 2)
BANK_C = (6, 4)


def tile_multiqueryattention_pa_t_kernel(
    tc, x, sin, cos, W_qkv_words, W_qkv_scales, out_0, out_1, out_2
):
    nc = tc.nc
    with ExitStack() as ctx:
        keep = ctx.enter_context(tc.tile_pool(name="keep", bufs=1))
        quant = ctx.enter_context(tc.tile_pool(name="quant", bufs=4))
        work = ctx.enter_context(tc.tile_pool(name="work", bufs=4))
        psum = ctx.enter_context(tc.psum_pool(name="psum", bufs=2))
        ctx.enter_context(tc.manual_schedule())

        w_scales = keep.tile([P, PASSES, N_QKV], U8, align_bytes=64)
        nc.vector.memset(w_scales[:].bitcast(I32), 0)

        sin_bf = keep.tile([P, ROWS, HD], BF16)
        cos_bf = keep.tile([P, ROWS, HD], BF16)

        def load_table_rows(j0, j1):
            for table_bf, table in ((cos_bf, cos), (sin_bf, sin)):
                nc.sync.dma_start(
                    out=table_bf[:, j0:j1, :], in_=table.rearrange("(p j) d -> p j d", j=ROWS)[:, j0:j1, :]
                )

        x_pairs = []

        def load_x_pair(s, pieces):
            b, j = divmod(PAIR * s, ROWS)
            x_sb = keep.tile([P, PAIR, D], BF16, name="x_sb%d" % s)
            x_pairs.append(x_sb)
            n = PAIR // pieces
            return [
                (x_sb[:, a : a + n, :], x[b].rearrange("(p j) k -> p j k", j=ROWS)[:, j + a : j + a + n, :])
                for a in range(0, PAIR, n)
            ]

        load_table_rows(0, FIRST_ROWS)
        first_x = load_x_pair(0, PAIR)
        nc.sync.dma_start(out=first_x[0][0], in_=first_x[0][1])

        scale_rows = W_qkv_scales.bitcast(I32).rearrange("g q n -> q g n")
        for quadrant in range(4):
            nc.sync.dma_start(
                out=w_scales[32 * quadrant : 32 * quadrant + 4].bitcast(I32),
                in_=scale_rows[4 * quadrant : 4 * quadrant + 4],
            )
        w_words = keep.tile([P, PASSES, 2 * N_QKV], U8, align_bytes=64)
        nc.sync.dma_start(
            out=w_words[:].bitcast(I32), in_=W_qkv_words.bitcast(I32).rearrange("g p n -> p g n")
        )
        nc.sync.dma_start(out=first_x[1][0], in_=first_x[1][1])
        load_table_rows(FIRST_ROWS, ROWS)
        for s in range(1, TILES // PAIR):
            for sb_side, hbm_side in load_x_pair(s, 1):
                nc.sync.dma_start(out=sb_side, in_=hbm_side)

        ident = keep.tile([P, P], F32)
        make_identity(nc, ident[:])

        tables = keep.tile([P, ROWS, 2, 3, HD], F32)

        def sin_halves():
            return ((0, HALF, 1.0), (HALF, 0, -1.0))

        def build_first_tables(j0, j1):
            n = j1 - j0
            nc.vector.tensor_scalar_mul(
                out=tables[:, j0:j1, 0, 0:2, :],
                in0=cos_bf[:, j0:j1, :].unsqueeze(2).to_broadcast([P, n, 2, HD]),
                scalar1=Q_SCALE,
            )
            nc.vector.tensor_copy(out=tables[:, j0:j1, 0, 2, :], in_=cos_bf[:, j0:j1, :])
            for lo, other, sign in sin_halves():
                nc.gpsimd.tensor_scalar(
                    out=tables[:, j0:j1, 1, 0:2, lo : lo + HALF],
                    in0=sin_bf[:, j0:j1, other : other + HALF].unsqueeze(2).to_broadcast([P, n, 2, HALF]),
                    scalar1=sign * Q_SCALE,
                    scalar2=0.0,
                    op0=MULT,
                    op1=ADD,
                )
                nc.gpsimd.tensor_scalar(
                    out=tables[:, j0:j1, 1, 2, lo : lo + HALF],
                    in0=sin_bf[:, j0:j1, other : other + HALF],
                    scalar1=sign,
                    scalar2=0.0,
                    op0=MULT,
                    op1=ADD,
                )

        def build_tables(j0, j1):
            n = j1 - j0
            nc.scalar.activation(
                out=tables[:, j0:j1, 0, 0:2, :],
                in_=cos_bf[:, j0:j1, :].unsqueeze(2).to_broadcast([P, n, 2, HD]),
                func=COPY,
                scale=Q_SCALE,
            )
            nc.scalar.copy(out=tables[:, j0:j1, 0, 2, :], in_=cos_bf[:, j0:j1, :])
            for lo, other, sign in sin_halves():
                nc.scalar.activation(
                    out=tables[:, j0:j1, 1, 0:2, lo : lo + HALF],
                    in_=sin_bf[:, j0:j1, other : other + HALF].unsqueeze(2).to_broadcast([P, n, 2, HALF]),
                    func=COPY,
                    scale=sign * Q_SCALE,
                )
                nc.scalar.activation(
                    out=tables[:, j0:j1, 1, 2, lo : lo + HALF],
                    in_=sin_bf[:, j0:j1, other : other + HALF],
                    func=COPY,
                    scale=sign,
                )

        grouped_of = {}
        codes_of = {}
        banks_of = {}
        out_of = {}

        def transpose_tile(i):
            x_words = x_pairs[i // PAIR][:, i % PAIR, :].bitcast(F32)
            xt = psum.tile([P, 2 * PASSES, P], F32)
            for g in range(PASSES):
                for u in range(2):
                    nc.tensor.transpose(
                        xt[:, 2 * g + u, :], x_words[:, 256 * g + u : 256 * (g + 1) : 2], ident[:]
                    )
            grouped = quant.tile([P, PASSES, P, 4], BF16, align_bytes=64)
            nc.scalar.copy(
                out=grouped[:]
                .rearrange("p g r t -> p (g r t)")
                .bitcast(F32)
                .rearrange("p (g r u) -> p g r u", g=PASSES, u=2),
                in_=xt[:].rearrange("p (g u) r -> p g r u", u=2),
            )
            grouped_of[i] = grouped

        def quantise_tile(i):
            codes = quant.tile([P, PASSES, P], U32, align_bytes=64)
            scales = quant.tile([P, PASSES, P], U8, align_bytes=64)
            nc.vector.quantize_mx(
                out=codes[:].rearrange("p g r -> p (g r)").bitcast(FP8X4),
                scales=scales[:].rearrange("p g r -> p (g r)"),
                in_=grouped_of[i][:].rearrange("p g r t -> p (g r t)"),
            )
            codes_of[i] = (codes, scales)

        def project(codes, scales, acc, col0, width):
            for g in range(PASSES):
                nc.tensor.matmul_mx(
                    out=acc,
                    lhsT=codes[:, g, :].bitcast(FP8X4),
                    lhsT_scale=scales[:, g, :],
                    rhs=w_words[:, g, 2 * col0 : 2 * (col0 + width)].bitcast(FP4X4),
                    rhs_scale=w_scales[:, g, col0 : col0 + width],
                    start=(g == 0),
                    stop=(g == PASSES - 1),
                )

        def project_tile(i):
            codes, scales = codes_of[i]
            bank_a = psum.tile([P, BANK_A[1], HD], F32)
            bank_b = psum.tile([P, BANK_B[1], HD], F32)
            bank_c = psum.tile([P, BANK_C[1], HD], F32)
            project(codes, scales, bank_a[:].rearrange("p h d -> p (h d)"), BANK_A[0] * HD, BANK_A[1] * HD)
            for h in range(BANK_B[1]):
                project(codes, scales, bank_b[:, h, :], (BANK_B[0] + h) * HD, HD)
            project(codes, scales, bank_c[:].rearrange("p h d -> p (h d)"), BANK_C[0] * HD, BANK_C[1] * HD)
            banks_of[i] = (bank_a, bank_b, bank_c)

        def open_pair(s):
            products = work.tile([P, 2, ROPE_HEADS + 1, PAIR, HD], F32)
            out_of[s] = products

        def copy_value_head(i):
            bank_c = banks_of[i][2]
            nc.scalar.copy(
                out=out_of[i // PAIR][:, 0, V_SLOT, i % PAIR, :], in_=bank_c[:, V_SLOT - BANK_C[0], :]
            )

        def rope_banks_ab(i):
            j = i % ROWS
            products = out_of[i // PAIR]
            bank_a, bank_b, bank_c = banks_of[i]
            for bank, (h0, n) in ((bank_a, BANK_A), (bank_b, BANK_B)):
                nc.vector.tensor_tensor(
                    out=products[:, :, h0 : h0 + n, i % PAIR, :],
                    in0=bank[:].unsqueeze(1).to_broadcast([P, 2, n, HD]),
                    in1=tables[:, j, :, 0, :].unsqueeze(2).to_broadcast([P, 2, n, HD]),
                    op=MULT,
                )

        def rope_bank_c(i):
            j = i % ROWS
            products = out_of[i // PAIR]
            bank_c = banks_of[i][2]
            nc.vector.tensor_tensor(
                out=products[:, :, BANK_C[0] : ROPE_HEADS, i % PAIR, :],
                in0=bank_c[:, 0:3, :].unsqueeze(1).to_broadcast([P, 2, 3, HD]),
                in1=tables[:, j, :, :, :],
                op=MULT,
            )

        def add_heads(i, adder, h0, h1):
            products = out_of[i // PAIR]
            first = products[:, 0, h0:h1, i % PAIR, :].rearrange("p h (e c) -> p h e c", e=2)
            second = products[:, 1, h0:h1, i % PAIR, :].rearrange("p h (e c) -> p h e c", e=2)
            adder.tensor_tensor(out=first, in0=first, in1=second[:, :, ::-1, :], op=ADD)

        def store_queries(i0, n, h0, h1):
            b, j = divmod(i0, ROWS)
            jj = i0 % PAIR
            nc.sync.dma_start(
                out=out_0[b].rearrange("h (p j) d -> p h j d", j=ROWS)[:, h0:h1, j : j + n, :],
                in_=out_of[i0 // PAIR][:, 0, h0:h1, jj : jj + n, :],
            )

        def store_single_head(i0, n, slot, out_hbm):
            b, j = divmod(i0, ROWS)
            jj = i0 % PAIR
            nc.sync.dma_start(
                out=out_hbm[b].rearrange("(p j) d -> p j d", j=ROWS)[:, j : j + n, :],
                in_=out_of[i0 // PAIR][:, 0, slot, jj : jj + n, :],
            )

        def store_tiles(i0, n):
            store_queries(i0, n, 0, H)
            store_single_head(i0, n, H, out_1)
            store_single_head(i0, n, V_SLOT, out_2)

        build_first_tables(0, FIRST_ROWS)
        transpose_tile(0)
        quantise_tile(0)
        transposed = 1
        quantised = 1
        table_rows = FIRST_ROWS
        for i in range(TILES):
            ready = transposed
            if i > 0:
                for t in range(quantised, min(i + 3, ready, quantised + 2, TILES)):
                    quantise_tile(t)
                    quantised = t + 1
            if i % PAIR == 0:
                open_pair(i // PAIR)
            project_tile(i)
            copy_value_head(i)
            for t in range(transposed, min(i + 4, transposed + 2, TILES)):
                transpose_tile(t)
                transposed = t + 1
            if table_rows < ROWS:
                build_tables(table_rows, table_rows + FIRST_ROWS)
                table_rows += FIRST_ROWS
            rope_banks_ab(i)
            if i == 0:
                quantise_tile(1)
                quantised = 2
            rope_bank_c(i)
            if i < TILES - VECTOR_ADD_TILES:
                add_heads(i, nc.gpsimd, 0, ROPE_HEADS)
                if i >= TILES - PAIR:
                    store_tiles(i, 1)
                elif i % PAIR == PAIR - 1:
                    store_tiles(i - PAIR + 1, PAIR)
            else:
                store_single_head(i, 1, V_SLOT, out_2)
                add_heads(i, nc.vector, 0, BANK_C[0])
                store_queries(i, 1, 0, BANK_C[0])
                add_heads(i, nc.vector, BANK_C[0], ROPE_HEADS)
                store_queries(i, 1, BANK_C[0], H)
                store_single_head(i, 1, H, out_1)
